import numpy as np
import ml_dtypes


def mxq(x, axis, fmt="e4m3"):
    dtype, down = {"e4m3": (ml_dtypes.float8_e4m3fn, 7), "e5m2": (ml_dtypes.float8_e5m2, 14)}[fmt]
    v = np.moveaxis(np.asarray(x, np.float32).astype(ml_dtypes.bfloat16).astype(np.float64), axis, -1)
    blocks = v.reshape(v.shape[:-1] + (-1, 32))
    amax = np.abs(blocks).max(-1, keepdims=True)
    byte = np.maximum(np.where(amax > 0, np.frexp(amax)[1] - 1 + 127, 0) - down, 1)
    scale = np.exp2(byte - 127.0)
    codes = (blocks / scale).astype(np.float32).astype(dtype).astype(np.float64)
    return np.moveaxis((codes * scale).reshape(v.shape), -1, axis)


WIDE = False


def mx_kscale(k):
    if not WIDE:
        return np.ones(k)
    levels = np.array([10, -10, 5, -5, 0])
    if k % 512:
        return np.exp2(np.random.permutation(np.resize(levels, k // 32))).repeat(32)
    a = np.empty((k // 512, 16))
    for p in range(k // 512):
        a[p, :8] = np.random.permutation(np.resize(levels, 8))
        for g in range(8):
            far = levels[np.abs(levels - a[p, g]) >= 10]
            a[p, g + 8] = far[np.random.randint(len(far))]
    return np.exp2(a.ravel()).repeat(32)


BF16 = ml_dtypes.bfloat16


def bf(x):
    return np.asarray(x, np.float32).astype(BF16)


def f64(x):
    return np.asarray(x).astype(np.float64)


N, C, H, W, B = 1024, 8, 4, 4, 8192
D = C * H * W


def setup_inputs():
    s = mx_kscale(N)
    sig = (0.5 + 0.5 * np.random.random((B, 1))) * (1.0 + np.random.random((B, 1)))
    z = np.random.standard_normal((B, N)) * sig
    e = np.exp(z - z.max(1, keepdims=True))
    w = e / e.sum(1, keepdims=True)
    memory = np.random.standard_normal((N, D)) * (0.5 + np.random.random((N, 1))) * 3.0
    add = np.random.standard_normal((B, C, H, W)) * 3.0 * np.sqrt(N / B)
    return {"w": bf(w * s), "memory": bf((memory / s[:, None]).reshape(N, C, H, W)), "add": bf(add / np.mean(s * s))}


def reference(w, memory, add):
    wf = f64(w)
    mem_flat = f64(memory).reshape(N, D)
    a = f64(add).reshape(B, D)
    new_memory = mem_flat + wf.T @ a
    r = mxq(wf, 1, "e4m3") @ mxq(new_memory, 0, "e4m3")
    return r.reshape(B, C, H, W)

@@ -1,0 +1,249 @@
+from contextlib import ExitStack
+
+import concourse.mybir as mybir
+from concourse.masks import make_identity
+
+F32 = mybir.dt.float32
+BF16 = mybir.dt.bfloat16
+U32 = mybir.dt.uint32
+U8 = mybir.dt.uint8
+FP8X4 = mybir.dt.float8_e4m3fn_x4
+
+P = 128
+KEYS = 8192
+SLOTS = 1024
+D = 128
+CHUNKS = KEYS // P
+HALF = 512
+GROUP = 4
+GROUPS = CHUNKS // GROUP
+FLOPS = 2 * 2 * KEYS * SLOTS * D
+
+W_SIZES = [1, 1, 2] + [4] * 11 + [2] * 6 + [1] * 4
+W_PLAN = [(sum(W_SIZES[:e]), W_SIZES[e]) for e in range(len(W_SIZES))]
+W_MAX = 4
+A_PLAN = [(0, 4), (4, 4)] + [(j, 8) for j in range(8, 64, 8)]
+M_PLAN = [(0, 4), (4, 4)]
+W_BUFS = 8
+AHEAD = W_BUFS - 1
+LATE = 4
+R_SIZES = [4] * 16
+R_PLAN = [(sum(R_SIZES[:b]), R_SIZES[b]) for b in range(len(R_SIZES))]
+LAST_QUANT_AFTER = 0
+O_BUFS = 12
+DUMMIES_A = 2
+DUMMIES_B = 1
+R_BANKS = [0, 1, 6, 7, 2, 3, 4, 5]
+R_ON_VECTOR = [0, 3, 5, 7, 9, 11, 13, 15, 17]
+
+
+def tile_memory_pb_t_kernel(tc, w, memory, add, out):
+    nc = tc.nc
+    w_rows = w.rearrange("(p j) n -> p (j n)", j=CHUNKS)
+    a_rows = add.rearrange("(p j) c h w -> p (j c h w)", j=CHUNKS)
+    o_rows = out.rearrange("(p j) c h w -> p (j c h w)", j=CHUNKS)
+    m_rows = memory.rearrange("(c p) a h w -> p c (a h w)", p=P)
+
+    with ExitStack() as ctx:
+        const = ctx.enter_context(tc.tile_pool(name="const", bufs=1))
+        keep = ctx.enter_context(tc.tile_pool(name="keep", bufs=1))
+        wpool = ctx.enter_context(tc.tile_pool(name="wpool", bufs=W_BUFS))
+        gpool = ctx.enter_context(tc.tile_pool(name="gpool", bufs=3))
+        opool = ctx.enter_context(tc.tile_pool(name="opool", bufs=O_BUFS))
+        psum = ctx.enter_context(tc.psum_pool(name="psum", bufs=1))
+        ctx.enter_context(tc.manual_schedule())
+
+        def bank(index, dtype):
+            return psum.tile([P, HALF], dtype, name="ps%d" % index, tag="b%d" % index)
+
+        ident_f = const.tile([P, P], F32, name="ident_f")
+        make_identity(nc, ident_f[:])
+        ident_b = const.tile([P, P], BF16, name="ident_b")
+        make_identity(nc, ident_b[:])
+
+        dma_order = []
+        for e in range(len(W_PLAN)):
+            j0 = W_PLAN[e][0]
+            for q in range(len(A_PLAN)):
+                if A_PLAN[q][0] == j0:
+                    dma_order.append(("a", q))
+            dma_order.append(("w", e))
+        for q in range(len(M_PLAN)):
+            dma_order.append(("m", q))
+        issued = [0]
+        w_of = {}
+        a_of = {}
+        m_of = {}
+
+        def issue_through(e_last):
+            while issued[0] < len(dma_order):
+                kind, index = dma_order[issued[0]]
+                if kind == "w" and index > e_last:
+                    break
+                issued[0] += 1
+                if kind == "w":
+                    j0, n = W_PLAN[index]
+                    w_t = wpool.tile([P, W_MAX * SLOTS], BF16, name="w_t", tag="w")
+                    nc.sync.dma_start(out=w_t[:, 0 : n * SLOTS], in_=w_rows[:, j0 * SLOTS : (j0 + n) * SLOTS])
+                    for r in range(n):
+                        w_of[j0 + r] = (w_t, r)
+                elif kind == "a":
+                    j0, n = A_PLAN[index]
+                    a_t = const.tile([P, n * D], BF16, name="a_t%d" % index)
+                    nc.sync.dma_start(out=a_t[:], in_=a_rows[:, j0 * D : (j0 + n) * D])
+                    for r in range(n):
+                        a_of[j0 + r] = (a_t, r)
+                else:
+                    c0, n = M_PLAN[index]
+                    m_t = const.tile([P, n, D], BF16, name="m_t%d" % index)
+                    nc.sync.dma_start(out=m_t[:], in_=m_rows[:, c0 : c0 + n, :])
+                    for r in range(n):
+                        m_of[c0 + r] = (m_t, r)
+
+        acc = [bank(0, F32), bank(1, F32)]
+        xt_of = {}
+        grouped_of = {}
+        codes = {}
+        scales = {}
+
+        def mm(i, h):
+            w_t, r = w_of[i]
+            a_t, ra = a_of[i]
+            nc.tensor.matmul(
+                out=acc[h][:],
+                lhsT=a_t[:, ra * D : (ra + 1) * D],
+                rhs=w_t[:, r * SLOTS + h * HALF : r * SLOTS + (h + 1) * HALF],
+                start=(i == 0),
+                stop=False,
+            )
+
+        def add_memory():
+            for c in range(SLOTS // P):
+                h, cc = divmod(c, HALF // P)
+                m_t, r = m_of[c]
+                nc.tensor.matmul(
+                    out=acc[h][:, cc * P : (cc + 1) * P],
+                    lhsT=m_t[:, r, :],
+                    rhs=ident_b[:],
+                    start=False,
+                    stop=(cc == HALF // P - 1),
+                )
+
+        def transposes(i, quarters):
+            w_t, r = w_of[i]
+            words = w_t[:].bitcast(F32)
+            if i not in xt_of:
+                xt_of[i] = bank(2 + i % 6, F32)
+            for c in quarters:
+                nc.tensor.transpose(
+                    out=xt_of[i][:, c * P : (c + 1) * P],
+                    in_=words[:, r * HALF + (c // 2) * 2 * P + c % 2 : r * HALF + (c // 2 + 1) * 2 * P : 2],
+                    identity=ident_f[:],
+                )
+
+        def evac(i):
+            k, r = divmod(i, GROUP)
+            if r == 0:
+                grouped_of[k] = gpool.tile([P, GROUP * SLOTS], BF16, name="grouped", tag="grouped", align_bytes=64)
+            dst = grouped_of[k][:].bitcast(F32)[:, r * HALF : (r + 1) * HALF].rearrange("p (g k u) -> p g k u", g=2, u=2)
+            src = xt_of[i][:].rearrange("p (g u k) -> p g k u", g=2, u=2)
+            if r == 0:
+                nc.vector.tensor_copy(out=dst, in_=src)
+            else:
+                nc.scalar.copy(out=dst, in_=src)
+
+        def quant(k):
+            codes[k] = keep.tile([P, GROUP * 2 * P], U32, name="codes%d" % k, align_bytes=64)
+            scales[k] = keep.tile([P, GROUP * 2 * P], U8, name="scales%d" % k, align_bytes=64)
+            nc.vector.quantize_mx(out=codes[k][:].bitcast(FP8X4), scales=scales[k][:], in_=grouped_of[k][:])
+
+        def dummies(index, count):
+            if count > 0:
+                d_t = bank(index, F32)
+                for q in range(count):
+                    nc.tensor.matmul(out=d_t[:], lhsT=ident_b[:], rhs=a_of[0][0][:], start=True, stop=True)
+
+        issue_through(AHEAD - 1)
+        entry_at = {}
+        for e in range(len(W_PLAN)):
+            entry_at[W_PLAN[e][0]] = e
+        for i in range(CHUNKS):
+            if i in entry_at:
+                issue_through(entry_at[i] + AHEAD)
+            if i < CHUNKS - LATE:
+                mm(i, 0)
+                transposes(i, [0, 1])
+                mm(i, 1)
+                transposes(i, [2, 3])
+                evac(i)
+                if i % GROUP == 0 and i >= GROUP:
+                    quant(i // GROUP - 1)
+            else:
+                mm(i, 0)
+                mm(i, 1)
+        add_memory()
+        quant(GROUPS - 2)
+
+        nm_t = []
+        for h in range(2):
+            nm_t.append(keep.tile([P, HALF], BF16, name="nm_t%d" % h))
+            dst = nm_t[h][:].rearrange("d (u e p) -> d u e p", u=2, e=2)
+            src = acc[h][:].rearrange("d (p u e) -> d u e p", u=2, e=2)
+            if h == 0:
+                nc.vector.tensor_copy(out=dst, in_=src)
+            else:
+                nc.scalar.copy(out=dst, in_=src)
+        dummies(2, DUMMIES_A)
+        nm_p = [bank(6, BF16), bank(7, BF16)]
+        for h in range(2):
+            for t in range(4):
+                nc.tensor.transpose(
+                    out=nm_p[h][:, t * P : (t + 1) * P],
+                    in_=nm_t[h][:, t * P : (t + 1) * P],
+                    identity=ident_b[:],
+                )
+        for i in range(CHUNKS - LATE, CHUNKS):
+            transposes(i, [0, 1, 2, 3])
+        dummies(1, DUMMIES_B)
+        nm_g = []
+        nm_c = []
+        nm_s = []
+        for h in range(2):
+            nm_g.append(keep.tile([P, HALF], BF16, name="nm_g%d" % h, align_bytes=64))
+            nm_c.append(keep.tile([P, P], U32, name="nm_c%d" % h, align_bytes=64))
+            nm_s.append(keep.tile([P, P], U8, name="nm_s%d" % h, align_bytes=64))
+            dst = nm_g[h][:].rearrange("p (d t) -> p d t", t=4)
+            src = nm_p[h][:].rearrange("p (t d) -> p d t", t=4)
+            if h == 0:
+                nc.scalar.copy(out=dst, in_=src)
+            else:
+                nc.vector.tensor_copy(out=dst, in_=src)
+        for h in range(2):
+            nc.vector.quantize_mx(out=nm_c[h][:].bitcast(FP8X4), scales=nm_s[h][:], in_=nm_g[h][:])
+        for i in range(CHUNKS - LATE, CHUNKS):
+            evac(i)
+
+        for b in range(len(R_PLAN)):
+            c0, n = R_PLAN[b]
+            r_t = bank(R_BANKS[b % 8], F32)
+            for jj in range(n):
+                k, r = divmod(c0 + jj, GROUP)
+                for g in range(2):
+                    col = (r * 2 + g) * P
+                    nc.tensor.matmul_mx(
+                        out=r_t[:, jj * P : (jj + 1) * P],
+                        lhsT=codes[k][:, col : col + P].bitcast(FP8X4),
+                        lhsT_scale=scales[k][:, col : col + P],
+                        rhs=nm_c[g][:].bitcast(FP8X4),
+                        rhs_scale=nm_s[g][:],
+                        start=(g == 0),
+                        stop=(g == 1),
+                    )
+            o_t = opool.tile([P, HALF], F32, name="o_t", tag="o")
+            if b in R_ON_VECTOR:
+                nc.vector.tensor_copy(out=o_t[:, 0 : n * D], in_=r_t[:, 0 : n * D])
+            else:
+                nc.scalar.copy(out=o_t[:, 0 : n * D], in_=r_t[:, 0 : n * D])
+            nc.sync.dma_start(out=o_rows[:, c0 * D : (c0 + n) * D], in_=o_t[:, 0 : n * D])
+            if b == LAST_QUANT_AFTER:
+                quant(GROUPS - 1)

@@ -24,13 +24,14 @@ W_PLAN = [(sum(W_SIZES[:e]), W_SIZES[e]) for e in range(len(W_SIZES))]
 W_MAX = 4
 A_PLAN = [(0, 4), (4, 4)] + [(j, 8) for j in range(8, 64, 8)]
 M_PLAN = [(0, 4), (4, 4)]
-W_BUFS = 8
+W_BUFS = 6
+PIECE = 2
 AHEAD = W_BUFS - 1
 LATE = 4
 R_SIZES = [4] * 16
 R_PLAN = [(sum(R_SIZES[:b]), R_SIZES[b]) for b in range(len(R_SIZES))]
 LAST_QUANT_AFTER = 0
-O_BUFS = 12
+O_BUFS = 10
 DUMMIES_A = 2
 DUMMIES_B = 1
 R_BANKS = [0, 1, 6, 7, 2, 3, 4, 5]
@@ -48,6 +49,7 @@ def tile_memory_pb_t_kernel(tc, w, memory, add, out):
         const = ctx.enter_context(tc.tile_pool(name="const", bufs=1))
         keep = ctx.enter_context(tc.tile_pool(name="keep", bufs=1))
         wpool = ctx.enter_context(tc.tile_pool(name="wpool", bufs=W_BUFS))
+        ppool = ctx.enter_context(tc.tile_pool(name="ppool", bufs=6))
         gpool = ctx.enter_context(tc.tile_pool(name="gpool", bufs=3))
         opool = ctx.enter_context(tc.tile_pool(name="opool", bufs=O_BUFS))
         psum = ctx.enter_context(tc.psum_pool(name="psum", bufs=1))
@@ -74,6 +76,7 @@ def tile_memory_pb_t_kernel(tc, w, memory, add, out):
         w_of = {}
         a_of = {}
         m_of = {}
+        p_of = {}
 
         def issue_through(e_last):
             while issued[0] < len(dma_order):
@@ -129,15 +132,27 @@ def tile_memory_pb_t_kernel(tc, w, memory, add, out):
                     stop=(cc == HALF // P - 1),
                 )
 
+        def permute(e):
+            j0, total = W_PLAN[e]
+            words = w_of[j0][0][:].bitcast(F32)
+            for lo in range(0, total, PIECE):
+                n = min(PIECE, total - lo)
+                p_t = ppool.tile([P, PIECE * HALF], F32, name="p_t", tag="p")
+                nc.vector.tensor_copy(
+                    out=p_t[:, 0 : n * HALF].rearrange("p (x u k) -> p x u k", u=2, k=P),
+                    in_=words[:, lo * HALF : (lo + n) * HALF].rearrange("p (x k u) -> p x u k", u=2, k=P),
+                )
+                for r in range(n):
+                    p_of[j0 + lo + r] = (p_t, r)
+
         def transposes(i, quarters):
-            w_t, r = w_of[i]
-            words = w_t[:].bitcast(F32)
+            p_t, r = p_of[i]
             if i not in xt_of:
                 xt_of[i] = bank(2 + i % 6, F32)
             for c in quarters:
                 nc.tensor.transpose(
                     out=xt_of[i][:, c * P : (c + 1) * P],
-                    in_=words[:, r * HALF + (c // 2) * 2 * P + c % 2 : r * HALF + (c // 2 + 1) * 2 * P : 2],
+                    in_=p_t[:, r * HALF + c * P : r * HALF + (c + 1) * P],
                     identity=ident_f[:],
                 )
 
@@ -147,10 +162,7 @@ def tile_memory_pb_t_kernel(tc, w, memory, add, out):
                 grouped_of[k] = gpool.tile([P, GROUP * SLOTS], BF16, name="grouped", tag="grouped", align_bytes=64)
             dst = grouped_of[k][:].bitcast(F32)[:, r * HALF : (r + 1) * HALF].rearrange("p (g k u) -> p g k u", g=2, u=2)
             src = xt_of[i][:].rearrange("p (g u k) -> p g k u", g=2, u=2)
-            if r == 0:
-                nc.vector.tensor_copy(out=dst, in_=src)
-            else:
-                nc.scalar.copy(out=dst, in_=src)
+            nc.scalar.copy(out=dst, in_=src)
 
         def quant(k):
             codes[k] = keep.tile([P, GROUP * 2 * P], U32, name="codes%d" % k, align_bytes=64)
@@ -170,17 +182,17 @@ def tile_memory_pb_t_kernel(tc, w, memory, add, out):
         for i in range(CHUNKS):
             if i in entry_at:
                 issue_through(entry_at[i] + AHEAD)
-            if i < CHUNKS - LATE:
-                mm(i, 0)
-                transposes(i, [0, 1])
-                mm(i, 1)
-                transposes(i, [2, 3])
-                evac(i)
-                if i % GROUP == 0 and i >= GROUP:
-                    quant(i // GROUP - 1)
-            else:
-                mm(i, 0)
-                mm(i, 1)
+                permute(entry_at[i])
+            j = i - LATE
+            mm(i, 0)
+            if j >= 0:
+                transposes(j, [0, 1])
+            mm(i, 1)
+            if j >= 0:
+                transposes(j, [2, 3])
+                evac(j)
+                if j % GROUP == 0 and j >= GROUP:
+                    quant(j // GROUP - 1)
         add_memory()
         quant(GROUPS - 2)
 

@@ -19,23 +19,23 @@ GROUP = 4
 GROUPS = CHUNKS // GROUP
 FLOPS = 2 * 2 * KEYS * SLOTS * D
 
-W_SIZES = [1, 1, 2] + [4] * 11 + [2] * 6 + [1] * 4
+W_SIZES = [1, 1, 1, 1, 2, 2, 2, 2] + [4] * 10 + [2] * 4 + [1] * 4
 W_PLAN = [(sum(W_SIZES[:e]), W_SIZES[e]) for e in range(len(W_SIZES))]
 W_MAX = 4
 A_PLAN = [(0, 4), (4, 4)] + [(j, 8) for j in range(8, 64, 8)]
 M_PLAN = [(0, 4), (4, 4)]
-W_BUFS = 6
+W_BUFS = 7
 PIECE = 2
 AHEAD = W_BUFS - 1
-LATE = 4
-R_SIZES = [4] * 16
+M_AT = 60
+M_ADD = 61
+LAG = 4
+LATE = 6
+WARM = 4
+R_SIZES = [4] * 15 + [2, 1, 1]
 R_PLAN = [(sum(R_SIZES[:b]), R_SIZES[b]) for b in range(len(R_SIZES))]
-LAST_QUANT_AFTER = 0
-O_BUFS = 10
-DUMMIES_A = 2
-DUMMIES_B = 1
-R_BANKS = [0, 1, 6, 7, 2, 3, 4, 5]
-R_ON_VECTOR = [0, 3, 5, 7, 9, 11, 13, 15, 17]
+O_BUFS = 8
+R_ON_VECTOR = [5, 7, 9, 11, 13, 14, 16]
 
 
 def tile_memory_pb_t_kernel(tc, w, memory, add, out):
@@ -49,7 +49,7 @@ def tile_memory_pb_t_kernel(tc, w, memory, add, out):
         const = ctx.enter_context(tc.tile_pool(name="const", bufs=1))
         keep = ctx.enter_context(tc.tile_pool(name="keep", bufs=1))
         wpool = ctx.enter_context(tc.tile_pool(name="wpool", bufs=W_BUFS))
-        ppool = ctx.enter_context(tc.tile_pool(name="ppool", bufs=6))
+        ppool = ctx.enter_context(tc.tile_pool(name="ppool", bufs=7))
         gpool = ctx.enter_context(tc.tile_pool(name="gpool", bufs=3))
         opool = ctx.enter_context(tc.tile_pool(name="opool", bufs=O_BUFS))
         psum = ctx.enter_context(tc.psum_pool(name="psum", bufs=1))
@@ -57,6 +57,12 @@ def tile_memory_pb_t_kernel(tc, w, memory, add, out):
 
         def bank(index, dtype):
             return psum.tile([P, HALF], dtype, name="ps%d" % index, tag="b%d" % index)
+
+        zeros = const.tile([P, HALF], BF16, name="zeros")
+        nc.vector.memset(zeros[:], 0.0)
+        warm = bank(7, F32)
+        for q in range(WARM):
+            nc.tensor.matmul(out=warm[:], lhsT=zeros[:, 0:P], rhs=zeros[:], start=True, stop=True)
 
         ident_f = const.tile([P, P], F32, name="ident_f")
         make_identity(nc, ident_f[:])
@@ -69,9 +75,10 @@ def tile_memory_pb_t_kernel(tc, w, memory, add, out):
             for q in range(len(A_PLAN)):
                 if A_PLAN[q][0] == j0:
                     dma_order.append(("a", q))
+            if j0 == M_AT:
+                for q in range(len(M_PLAN)):
+                    dma_order.append(("m", q))
             dma_order.append(("w", e))
-        for q in range(len(M_PLAN)):
-            dma_order.append(("m", q))
         issued = [0]
         w_of = {}
         a_of = {}
@@ -117,7 +124,7 @@ def tile_memory_pb_t_kernel(tc, w, memory, add, out):
                 lhsT=a_t[:, ra * D : (ra + 1) * D],
                 rhs=w_t[:, r * SLOTS + h * HALF : r * SLOTS + (h + 1) * HALF],
                 start=(i == 0),
-                stop=False,
+                stop=(i == CHUNKS - 1),
             )
 
         def add_memory():
@@ -129,7 +136,7 @@ def tile_memory_pb_t_kernel(tc, w, memory, add, out):
                     lhsT=m_t[:, r, :],
                     rhs=ident_b[:],
                     start=False,
-                    stop=(cc == HALF // P - 1),
+                    stop=False,
                 )
 
         def permute(e):
@@ -156,24 +163,21 @@ def tile_memory_pb_t_kernel(tc, w, memory, add, out):
                     identity=ident_f[:],
                 )
 
-        def evac(i):
+        def evac(i, on_vector=False):
             k, r = divmod(i, GROUP)
             if r == 0:
                 grouped_of[k] = gpool.tile([P, GROUP * SLOTS], BF16, name="grouped", tag="grouped", align_bytes=64)
             dst = grouped_of[k][:].bitcast(F32)[:, r * HALF : (r + 1) * HALF].rearrange("p (g k u) -> p g k u", g=2, u=2)
             src = xt_of[i][:].rearrange("p (g u k) -> p g k u", g=2, u=2)
-            nc.scalar.copy(out=dst, in_=src)
+            if on_vector:
+                nc.vector.tensor_copy(out=dst, in_=src)
+            else:
+                nc.scalar.copy(out=dst, in_=src)
 
         def quant(k):
-            codes[k] = keep.tile([P, GROUP * 2 * P], U32, name="codes%d" % k, align_bytes=64)
-            scales[k] = keep.tile([P, GROUP * 2 * P], U8, name="scales%d" % k, align_bytes=64)
+            codes[k] = keep.tile([P, GROUP * 2 * P], U32, name="codes%d" % k, align_bytes=256)
+            scales[k] = keep.tile([P, GROUP * 2 * P], U8, name="scales%d" % k, align_bytes=256)
             nc.vector.quantize_mx(out=codes[k][:].bitcast(FP8X4), scales=scales[k][:], in_=grouped_of[k][:])
-
-        def dummies(index, count):
-            if count > 0:
-                d_t = bank(index, F32)
-                for q in range(count):
-                    nc.tensor.matmul(out=d_t[:], lhsT=ident_b[:], rhs=a_of[0][0][:], start=True, stop=True)
 
         issue_through(AHEAD - 1)
         entry_at = {}
@@ -183,61 +187,73 @@ def tile_memory_pb_t_kernel(tc, w, memory, add, out):
             if i in entry_at:
                 issue_through(entry_at[i] + AHEAD)
                 permute(entry_at[i])
-            j = i - LATE
-            mm(i, 0)
-            if j >= 0:
-                transposes(j, [0, 1])
-            mm(i, 1)
-            if j >= 0:
-                transposes(j, [2, 3])
+            if i == M_ADD:
+                add_memory()
+            j = i - LAG
+            for h in range(2):
+                mm(i, h)
+                if 0 <= j < CHUNKS - LATE:
+                    transposes(j, [2 * h, 2 * h + 1])
+            if 0 <= j < CHUNKS - LATE:
                 evac(j)
                 if j % GROUP == 0 and j >= GROUP:
                     quant(j // GROUP - 1)
-        add_memory()
-        quant(GROUPS - 2)
 
-        nm_t = []
-        for h in range(2):
-            nm_t.append(keep.tile([P, HALF], BF16, name="nm_t%d" % h))
+        nm_t = [keep.tile([P, HALF], BF16, name="nm_t%d" % h) for h in range(2)]
+        nm_g = [keep.tile([P, HALF], BF16, name="nm_g%d" % h, align_bytes=64) for h in range(2)]
+        nm_c = [keep.tile([P, P], U32, name="nm_c%d" % h, align_bytes=64) for h in range(2)]
+        nm_s = [keep.tile([P, P], U8, name="nm_s%d" % h, align_bytes=64) for h in range(2)]
+        nm_p = {}
+
+        def nm_round(h, on_vector):
             dst = nm_t[h][:].rearrange("d (u e p) -> d u e p", u=2, e=2)
             src = acc[h][:].rearrange("d (p u e) -> d u e p", u=2, e=2)
-            if h == 0:
+            if on_vector:
                 nc.vector.tensor_copy(out=dst, in_=src)
             else:
                 nc.scalar.copy(out=dst, in_=src)
-        dummies(2, DUMMIES_A)
-        nm_p = [bank(6, BF16), bank(7, BF16)]
-        for h in range(2):
+
+        def nm_transposes(h):
+            nm_p[h] = bank(h, BF16)
             for t in range(4):
                 nc.tensor.transpose(
                     out=nm_p[h][:, t * P : (t + 1) * P],
                     in_=nm_t[h][:, t * P : (t + 1) * P],
                     identity=ident_b[:],
                 )
-        for i in range(CHUNKS - LATE, CHUNKS):
-            transposes(i, [0, 1, 2, 3])
-        dummies(1, DUMMIES_B)
-        nm_g = []
-        nm_c = []
-        nm_s = []
-        for h in range(2):
-            nm_g.append(keep.tile([P, HALF], BF16, name="nm_g%d" % h, align_bytes=64))
-            nm_c.append(keep.tile([P, P], U32, name="nm_c%d" % h, align_bytes=64))
-            nm_s.append(keep.tile([P, P], U8, name="nm_s%d" % h, align_bytes=64))
-            dst = nm_g[h][:].rearrange("p (d t) -> p d t", t=4)
-            src = nm_p[h][:].rearrange("p (t d) -> p d t", t=4)
-            if h == 0:
-                nc.scalar.copy(out=dst, in_=src)
-            else:
-                nc.vector.tensor_copy(out=dst, in_=src)
-        for h in range(2):
-            nc.vector.quantize_mx(out=nm_c[h][:].bitcast(FP8X4), scales=nm_s[h][:], in_=nm_g[h][:])
-        for i in range(CHUNKS - LATE, CHUNKS):
-            evac(i)
 
+        def nm_group(h, on_vector):
+            dst = nm_g[h][:].rearrange("p (d t) -> p d t", t=4)
+            src = nm_p[h][:, 0:HALF].rearrange("p (t d) -> p d t", t=4)
+            if on_vector:
+                nc.vector.tensor_copy(out=dst, in_=src)
+            else:
+                nc.scalar.copy(out=dst, in_=src)
+
+        def nm_quant(h):
+            nc.vector.quantize_mx(out=nm_c[h][:].bitcast(FP8X4), scales=nm_s[h][:], in_=nm_g[h][:])
+
+        nm_round(0, True)
+        nm_round(1, False)
+        late = list(range(CHUNKS - LATE, CHUNKS))
+        for i in late[:2]:
+            transposes(i, [0, 1, 2, 3])
+        nm_transposes(0)
+        nm_transposes(1)
+        nm_group(0, True)
+        nm_group(1, False)
+        for i in late[2:]:
+            transposes(i, [0, 1, 2, 3])
+        nm_quant(0)
+        nm_quant(1)
+        for i in late:
+            evac(i, on_vector=(i >= CHUNKS - 3))
+        quant(GROUPS - 2)
+
+        r_banks = [0, 1] + [2 + (i % 6) for i in range(CHUNKS - 6, CHUNKS)]
         for b in range(len(R_PLAN)):
             c0, n = R_PLAN[b]
-            r_t = bank(R_BANKS[b % 8], F32)
+            r_t = bank(r_banks[b % 8], F32)
             for jj in range(n):
                 k, r = divmod(c0 + jj, GROUP)
                 for g in range(2):
@@ -257,5 +273,5 @@ def tile_memory_pb_t_kernel(tc, w, memory, add, out):
             else:
                 nc.scalar.copy(out=o_t[:, 0 : n * D], in_=r_t[:, 0 : n * D])
             nc.sync.dma_start(out=o_rows[:, c0 * D : (c0 + n) * D], in_=o_t[:, 0 : n * D])
-            if b == LAST_QUANT_AFTER:
+            if b == 0:
                 quant(GROUPS - 1)

from contextlib import ExitStack

import concourse.mybir as mybir
from concourse.masks import make_identity

F32 = mybir.dt.float32
BF16 = mybir.dt.bfloat16
U32 = mybir.dt.uint32
U8 = mybir.dt.uint8
FP8X4 = mybir.dt.float8_e4m3fn_x4

P = 128
KEYS = 8192
SLOTS = 1024
D = 128
CHUNKS = KEYS // P
HALF = 512
GROUP = 4
GROUPS = CHUNKS // GROUP
FLOPS = 2 * 2 * KEYS * SLOTS * D

W_SIZES = [1, 1, 1, 1, 2, 2, 2, 2] + [4] * 10 + [2] * 4 + [1] * 4
W_PLAN = [(sum(W_SIZES[:e]), W_SIZES[e]) for e in range(len(W_SIZES))]
W_MAX = 4
A_PLAN = [(0, 4), (4, 4)] + [(j, 8) for j in range(8, 64, 8)]
M_PLAN = [(0, 4), (4, 4)]
W_BUFS = 7
PIECE = 2
AHEAD = W_BUFS - 1
M_AT = 60
M_ADD = 61
LAG = 4
LATE = 6
WARM = 4
R_SIZES = [4] * 15 + [2, 1, 1]
R_PLAN = [(sum(R_SIZES[:b]), R_SIZES[b]) for b in range(len(R_SIZES))]
O_BUFS = 8
R_ON_VECTOR = [5, 7, 9, 11, 13, 14, 16]


def tile_memory_pb_t_kernel(tc, w, memory, add, out):
    nc = tc.nc
    w_rows = w.rearrange("(p j) n -> p (j n)", j=CHUNKS)
    a_rows = add.rearrange("(p j) c h w -> p (j c h w)", j=CHUNKS)
    o_rows = out.rearrange("(p j) c h w -> p (j c h w)", j=CHUNKS)
    m_rows = memory.rearrange("(c p) a h w -> p c (a h w)", p=P)

    with ExitStack() as ctx:
        const = ctx.enter_context(tc.tile_pool(name="const", bufs=1))
        keep = ctx.enter_context(tc.tile_pool(name="keep", bufs=1))
        wpool = ctx.enter_context(tc.tile_pool(name="wpool", bufs=W_BUFS))
        ppool = ctx.enter_context(tc.tile_pool(name="ppool", bufs=7))
        gpool = ctx.enter_context(tc.tile_pool(name="gpool", bufs=3))
        opool = ctx.enter_context(tc.tile_pool(name="opool", bufs=O_BUFS))
        psum = ctx.enter_context(tc.psum_pool(name="psum", bufs=1))
        ctx.enter_context(tc.manual_schedule())

        def bank(index, dtype):
            return psum.tile([P, HALF], dtype, name="ps%d" % index, tag="b%d" % index)

        zeros = const.tile([P, HALF], BF16, name="zeros")
        nc.vector.memset(zeros[:], 0.0)
        warm = bank(7, F32)
        for q in range(WARM):
            nc.tensor.matmul(out=warm[:], lhsT=zeros[:, 0:P], rhs=zeros[:], start=True, stop=True)

        ident_f = const.tile([P, P], F32, name="ident_f")
        make_identity(nc, ident_f[:])
        ident_b = const.tile([P, P], BF16, name="ident_b")
        make_identity(nc, ident_b[:])

        dma_order = []
        for e in range(len(W_PLAN)):
            j0 = W_PLAN[e][0]
            for q in range(len(A_PLAN)):
                if A_PLAN[q][0] == j0:
                    dma_order.append(("a", q))
            if j0 == M_AT:
                for q in range(len(M_PLAN)):
                    dma_order.append(("m", q))
            dma_order.append(("w", e))
        issued = [0]
        w_of = {}
        a_of = {}
        m_of = {}
        p_of = {}

        def issue_through(e_last):
            while issued[0] < len(dma_order):
                kind, index = dma_order[issued[0]]
                if kind == "w" and index > e_last:
                    break
                issued[0] += 1
                if kind == "w":
                    j0, n = W_PLAN[index]
                    w_t = wpool.tile([P, W_MAX * SLOTS], BF16, name="w_t", tag="w")
                    nc.sync.dma_start(out=w_t[:, 0 : n * SLOTS], in_=w_rows[:, j0 * SLOTS : (j0 + n) * SLOTS])
                    for r in range(n):
                        w_of[j0 + r] = (w_t, r)
                elif kind == "a":
                    j0, n = A_PLAN[index]
                    a_t = const.tile([P, n * D], BF16, name="a_t%d" % index)
                    nc.sync.dma_start(out=a_t[:], in_=a_rows[:, j0 * D : (j0 + n) * D])
                    for r in range(n):
                        a_of[j0 + r] = (a_t, r)
                else:
                    c0, n = M_PLAN[index]
                    m_t = const.tile([P, n, D], BF16, name="m_t%d" % index)
                    nc.sync.dma_start(out=m_t[:], in_=m_rows[:, c0 : c0 + n, :])
                    for r in range(n):
                        m_of[c0 + r] = (m_t, r)

        acc = [bank(0, F32), bank(1, F32)]
        xt_of = {}
        grouped_of = {}
        codes = {}
        scales = {}

        def mm(i, h):
            w_t, r = w_of[i]
            a_t, ra = a_of[i]
            nc.tensor.matmul(
                out=acc[h][:],
                lhsT=a_t[:, ra * D : (ra + 1) * D],
                rhs=w_t[:, r * SLOTS + h * HALF : r * SLOTS + (h + 1) * HALF],
                start=(i == 0),
                stop=(i == CHUNKS - 1),
            )

        def add_memory():
            for c in range(SLOTS // P):
                h, cc = divmod(c, HALF // P)
                m_t, r = m_of[c]
                nc.tensor.matmul(
                    out=acc[h][:, cc * P : (cc + 1) * P],
                    lhsT=m_t[:, r, :],
                    rhs=ident_b[:],
                    start=False,
                    stop=False,
                )

        def permute(e):
            j0, total = W_PLAN[e]
            words = w_of[j0][0][:].bitcast(F32)
            for lo in range(0, total, PIECE):
                n = min(PIECE, total - lo)
                p_t = ppool.tile([P, PIECE * HALF], F32, name="p_t", tag="p")
                nc.vector.tensor_copy(
                    out=p_t[:, 0 : n * HALF].rearrange("p (x u k) -> p x u k", u=2, k=P),
                    in_=words[:, lo * HALF : (lo + n) * HALF].rearrange("p (x k u) -> p x u k", u=2, k=P),
                )
                for r in range(n):
                    p_of[j0 + lo + r] = (p_t, r)

        def transposes(i, quarters):
            p_t, r = p_of[i]
            if i not in xt_of:
                xt_of[i] = bank(2 + i % 6, F32)
            for c in quarters:
                nc.tensor.transpose(
                    out=xt_of[i][:, c * P : (c + 1) * P],
                    in_=p_t[:, r * HALF + c * P : r * HALF + (c + 1) * P],
                    identity=ident_f[:],
                )

        def evac(i, on_vector=False):
            k, r = divmod(i, GROUP)
            if r == 0:
                grouped_of[k] = gpool.tile([P, GROUP * SLOTS], BF16, name="grouped", tag="grouped", align_bytes=64)
            dst = grouped_of[k][:].bitcast(F32)[:, r * HALF : (r + 1) * HALF].rearrange("p (g k u) -> p g k u", g=2, u=2)
            src = xt_of[i][:].rearrange("p (g u k) -> p g k u", g=2, u=2)
            if on_vector:
                nc.vector.tensor_copy(out=dst, in_=src)
            else:
                nc.scalar.copy(out=dst, in_=src)

        def quant(k):
            codes[k] = keep.tile([P, GROUP * 2 * P], U32, name="codes%d" % k, align_bytes=256)
            scales[k] = keep.tile([P, GROUP * 2 * P], U8, name="scales%d" % k, align_bytes=256)
            nc.vector.quantize_mx(out=codes[k][:].bitcast(FP8X4), scales=scales[k][:], in_=grouped_of[k][:])

        issue_through(AHEAD - 1)
        entry_at = {}
        for e in range(len(W_PLAN)):
            entry_at[W_PLAN[e][0]] = e
        for i in range(CHUNKS):
            if i in entry_at:
                issue_through(entry_at[i] + AHEAD)
                permute(entry_at[i])
            if i == M_ADD:
                add_memory()
            j = i - LAG
            for h in range(2):
                mm(i, h)
                if 0 <= j < CHUNKS - LATE:
                    transposes(j, [2 * h, 2 * h + 1])
            if 0 <= j < CHUNKS - LATE:
                evac(j)
                if j % GROUP == 0 and j >= GROUP:
                    quant(j // GROUP - 1)

        nm_t = [keep.tile([P, HALF], BF16, name="nm_t%d" % h) for h in range(2)]
        nm_g = [keep.tile([P, HALF], BF16, name="nm_g%d" % h, align_bytes=64) for h in range(2)]
        nm_c = [keep.tile([P, P], U32, name="nm_c%d" % h, align_bytes=64) for h in range(2)]
        nm_s = [keep.tile([P, P], U8, name="nm_s%d" % h, align_bytes=64) for h in range(2)]
        nm_p = {}

        def nm_round(h, on_vector):
            dst = nm_t[h][:].rearrange("d (u e p) -> d u e p", u=2, e=2)
            src = acc[h][:].rearrange("d (p u e) -> d u e p", u=2, e=2)
            if on_vector:
                nc.vector.tensor_copy(out=dst, in_=src)
            else:
                nc.scalar.copy(out=dst, in_=src)

        def nm_transposes(h):
            nm_p[h] = bank(h, BF16)
            for t in range(4):
                nc.tensor.transpose(
                    out=nm_p[h][:, t * P : (t + 1) * P],
                    in_=nm_t[h][:, t * P : (t + 1) * P],
                    identity=ident_b[:],
                )

        def nm_group(h, on_vector):
            dst = nm_g[h][:].rearrange("p (d t) -> p d t", t=4)
            src = nm_p[h][:, 0:HALF].rearrange("p (t d) -> p d t", t=4)
            if on_vector:
                nc.vector.tensor_copy(out=dst, in_=src)
            else:
                nc.scalar.copy(out=dst, in_=src)

        def nm_quant(h):
            nc.vector.quantize_mx(out=nm_c[h][:].bitcast(FP8X4), scales=nm_s[h][:], in_=nm_g[h][:])

        nm_round(0, True)
        nm_round(1, False)
        late = list(range(CHUNKS - LATE, CHUNKS))
        for i in late[:2]:
            transposes(i, [0, 1, 2, 3])
        nm_transposes(0)
        nm_transposes(1)
        nm_group(0, True)
        nm_group(1, False)
        for i in late[2:]:
            transposes(i, [0, 1, 2, 3])
        nm_quant(0)
        nm_quant(1)
        for i in late:
            evac(i, on_vector=(i >= CHUNKS - 3))
        quant(GROUPS - 2)

        r_banks = [0, 1] + [2 + (i % 6) for i in range(CHUNKS - 6, CHUNKS)]
        for b in range(len(R_PLAN)):
            c0, n = R_PLAN[b]
            r_t = bank(r_banks[b % 8], F32)
            for jj in range(n):
                k, r = divmod(c0 + jj, GROUP)
                for g in range(2):
                    col = (r * 2 + g) * P
                    nc.tensor.matmul_mx(
                        out=r_t[:, jj * P : (jj + 1) * P],
                        lhsT=codes[k][:, col : col + P].bitcast(FP8X4),
                        lhsT_scale=scales[k][:, col : col + P],
                        rhs=nm_c[g][:].bitcast(FP8X4),
                        rhs_scale=nm_s[g][:],
                        start=(g == 0),
                        stop=(g == 1),
                    )
            o_t = opool.tile([P, HALF], F32, name="o_t", tag="o")
            if b in R_ON_VECTOR:
                nc.vector.tensor_copy(out=o_t[:, 0 : n * D], in_=r_t[:, 0 : n * D])
            else:
                nc.scalar.copy(out=o_t[:, 0 : n * D], in_=r_t[:, 0 : n * D])
            nc.sync.dma_start(out=o_rows[:, c0 * D : (c0 + n) * D], in_=o_t[:, 0 : n * D])
            if b == 0:
                quant(GROUPS - 1)
